import numpy as np
import ml_dtypes

BF16 = ml_dtypes.bfloat16


def bf(x):
    return np.asarray(x, np.float32).astype(BF16)


def f32(x):
    return np.asarray(x, np.float32)


def f64(x):
    return np.asarray(x).astype(np.float64)


def striped(idx):
    return np.tile(idx.reshape(-1, 16).T, (8, 1))


DN, DE, DG, L, C, S, N = 128, 128, 128, 768, 1024, 2048, 1024
DI = DN + DN + DE + DG


def setup_inputs():
    return {
        "base": f32(np.random.standard_normal((C, S))),
        "receiver": bf(np.random.standard_normal((DN, N))),
        "sender": bf(np.random.standard_normal((DN, N))),
        "edge_attr": bf(np.random.standard_normal((DE, N))),
        "global_attr": bf(np.random.standard_normal((DG, 1))),
        "w1": bf(np.random.standard_normal((DI, L)) / np.sqrt(DI)),
        "b1": f32(0.1 * np.random.standard_normal((L, 1))),
        "w2": bf(np.random.standard_normal((L, L)) * np.sqrt(2.0 / L)),
        "b2": f32(0.1 * np.random.standard_normal((L, 1))),
        "w3": bf(np.random.standard_normal((L, L)) * np.sqrt(2.0 / L)),
        "b3": f32(0.1 * np.random.standard_normal((L, 1))),
        "w4": bf(np.random.standard_normal((L, C)) * np.sqrt(2.0 / L)),
        "b4": f32(0.1 * np.random.standard_normal((C, 1))),
        "offs": striped(np.random.permutation(S)[:N]),
    }


def reference(base, receiver, sender, edge_attr, global_attr, w1, b1, w2, b2, w3, b3, w4, b4, offs):
    idx = offs[:16].T.reshape(-1)
    x = np.concatenate([f64(receiver), f64(sender), f64(edge_attr), np.tile(f64(global_attr), (1, N))], axis=0)
    h = np.maximum(f64(w1).T @ x + f64(b1), 0.0)
    h = np.maximum(f64(w2).T @ h + f64(b2), 0.0)
    h = np.maximum(f64(w3).T @ h + f64(b3), 0.0)
    out = f64(base).copy()
    out[:, idx] = f64(w4).T @ h + f64(b4)
    return out

@@ -1,0 +1,150 @@
+import concourse.mybir as mybir
+from concourse.masks import make_identity
+
+FP32 = mybir.dt.float32
+BF16 = mybir.dt.bfloat16
+U16 = mybir.dt.uint16
+ADD = mybir.AluOpType.add
+MAX = mybir.AluOpType.max
+RELU = mybir.ActivationFunctionType.Relu
+COPY = mybir.ActivationFunctionType.Copy
+
+P = 128
+N = 1024
+S = 2048
+L = 768
+C = 1024
+DI = 512
+HALF = 512
+
+FLOPS = 2 * N * (DI * L + L * L + L * L + L * C)
+
+
+def load_row_blocks(nc, pool, matrix, name):
+    rows, columns = matrix.shape
+    blocks = []
+    for k in range(rows // P):
+        block = pool.tile([P, columns], matrix.dtype, name=f"{name}_{k}")
+        nc.sync.dma_start(block[:], matrix[k * P : (k + 1) * P, :])
+        blocks.append(block)
+    return blocks
+
+
+def hidden_layer(nc, banks, pool, weights, halves, bias, name):
+    outputs = []
+    for i, blocks in enumerate(halves):
+        outputs.append([])
+        for m in range(L // P):
+            acc = banks.tile([P, HALF], FP32, name="acc")
+            for k, (weight, block) in enumerate(zip(weights, blocks)):
+                nc.tensor.matmul(
+                    acc[:],
+                    weight[:, m * P : (m + 1) * P],
+                    block,
+                    start=(k == 0),
+                    stop=(k == len(blocks) - 1),
+                )
+            hidden = pool.tile([P, HALF], BF16, name=f"{name}_{i}_{m}")
+            if m % 2 == 0:
+                nc.scalar.activation(hidden[:], acc[:], RELU, bias=bias[:, m : m + 1])
+            else:
+                nc.vector.tensor_scalar(hidden[:], acc[:], bias[:, m : m + 1], 0.0, ADD, MAX)
+            outputs[i].append(hidden[:])
+    return outputs
+
+
+def tile_edgemodel_b_kernel(
+    tc, base, receiver, sender, edge_attr, global_attr, w1, b1, w2, b2, w3, b3, w4, b4, offs, out
+):
+    nc = tc.nc
+    with (
+        tc.tile_pool(name="lists", bufs=1) as lists,
+        tc.tile_pool(name="held", bufs=1) as held,
+        tc.psum_pool(name="setup", bufs=1) as setup,
+        tc.psum_pool(name="banks", bufs=6) as banks,
+    ):
+        bias_rows = held.tile([P, P], FP32, name="bias_rows")
+        nc.vector.memset(bias_rows[:], 0.0)
+
+        offsets = lists.tile([P, N // 16], U16, name="offsets")
+        nc.sync.dma_start(offsets[:], offs)
+
+        features = []
+        for name, source in (("receiver", receiver), ("sender", sender), ("edge", edge_attr)):
+            feature = held.tile([P, N], BF16, name=name)
+            nc.sync.dma_start(feature[:], source)
+            features.append(feature)
+        w1_blocks = load_row_blocks(nc, held, w1, "w1")
+        global_column = held.tile([P, 1], BF16, name="global_column")
+        nc.sync.dma_start(global_column[:], global_attr)
+
+        first_row = {}
+        rows_used = 0
+        for name, vector in (("b1", b1), ("b2", b2), ("b3", b3), ("b4", b4)):
+            blocks = vector.shape[0] // P
+            nc.sync.dma_start(
+                bias_rows[rows_used : rows_used + blocks, :],
+                vector.rearrange("(m p) o -> m (p o)", p=P),
+            )
+            first_row[name] = rows_used
+            rows_used += blocks
+
+        w2_blocks = load_row_blocks(nc, held, w2, "w2")
+        w3_blocks = load_row_blocks(nc, held, w3, "w3")
+        w4_blocks = load_row_blocks(nc, held, w4, "w4")
+        windows = load_row_blocks(nc, held, base, "window")
+
+        identity = held.tile([P, P], FP32, name="identity")
+        make_identity(nc, identity[:])
+        bias_psum = setup.tile([P, P], FP32, name="bias_psum")
+        nc.tensor.transpose(bias_psum[:], bias_rows[:], identity[:])
+        bias = held.tile([P, P], FP32, name="bias")
+        nc.vector.tensor_copy(bias[:], bias_psum[:])
+
+        def bias_columns(name, count):
+            return bias[:, first_row[name] : first_row[name] + count]
+
+        global_psum = setup.tile([P, L // P], FP32, name="global_psum")
+        for m in range(L // P):
+            nc.tensor.matmul(
+                global_psum[:, m : m + 1],
+                w1_blocks[3][:, m * P : (m + 1) * P],
+                global_column[:],
+                start=True,
+                stop=True,
+            )
+        bias1 = held.tile([P, L // P], FP32, name="bias1")
+        nc.vector.tensor_tensor(bias1[:], global_psum[:], bias_columns("b1", L // P), ADD)
+
+        b4_columns = bias_columns("b4", C // P)
+        b4_wide = []
+        for c in range(C // P):
+            wide = held.tile([P, N], FP32, name=f"b4_wide_{c}")
+            nc.gpsimd.tensor_copy(wide[:], b4_columns[:, c : c + 1].to_broadcast([P, N]))
+            b4_wide.append(wide)
+
+        x_halves = [[f[:, i * HALF : (i + 1) * HALF] for f in features] for i in range(2)]
+        h1 = hidden_layer(nc, banks, held, w1_blocks[0:3], x_halves, bias1, "h1")
+        h2 = hidden_layer(nc, banks, held, w2_blocks, h1, bias_columns("b2", L // P), "h2")
+        h3 = hidden_layer(nc, banks, held, w3_blocks, h2, bias_columns("b3", L // P), "h3")
+
+        for c in range(C // P):
+            y = held.tile([P, N], FP32, name=f"y_{c}")
+            for i in range(2):
+                acc = banks.tile([P, HALF], FP32, name="acc")
+                for k in range(L // P):
+                    nc.tensor.matmul(
+                        acc[:],
+                        w4_blocks[k][:, c * P : (c + 1) * P],
+                        h3[i][k],
+                        start=(k == 0),
+                        stop=(k == L // P - 1),
+                    )
+                nc.scalar.activation(y[:, i * HALF : (i + 1) * HALF], acc[:], COPY)
+            nc.vector.tensor_tensor(
+                windows[c][:].indirect(offsets[:]),
+                y[:],
+                b4_wide[c][:],
+                ADD,
+            )
+            nc.sync.dma_start(out[c * P : (c + 1) * P, :], windows[c][:])

@@ -63,35 +63,41 @@ def tile_edgemodel_b_kernel(
         tc.psum_pool(name="setup", bufs=1) as setup,
         tc.psum_pool(name="banks", bufs=6) as banks,
     ):
+        global_column = held.tile([P, 1], BF16, name="global_column")
+        nc.scalar.dma_start(global_column[:], global_attr)
+
         bias_rows = held.tile([P, P], FP32, name="bias_rows")
         nc.vector.memset(bias_rows[:], 0.0)
-
-        offsets = lists.tile([P, N // 16], U16, name="offsets")
-        nc.sync.dma_start(offsets[:], offs)
-
-        features = []
-        for name, source in (("receiver", receiver), ("sender", sender), ("edge", edge_attr)):
-            feature = held.tile([P, N], BF16, name=name)
-            nc.sync.dma_start(feature[:], source)
-            features.append(feature)
-        w1_blocks = load_row_blocks(nc, held, w1, "w1")
-        global_column = held.tile([P, 1], BF16, name="global_column")
-        nc.sync.dma_start(global_column[:], global_attr)
-
         first_row = {}
         rows_used = 0
         for name, vector in (("b1", b1), ("b2", b2), ("b3", b3), ("b4", b4)):
             blocks = vector.shape[0] // P
-            nc.sync.dma_start(
+            nc.scalar.dma_start(
                 bias_rows[rows_used : rows_used + blocks, :],
                 vector.rearrange("(m p) o -> m (p o)", p=P),
             )
             first_row[name] = rows_used
             rows_used += blocks
 
+        w1_global = held.tile([P, L], BF16, name="w1_global")
+        nc.sync.dma_start(w1_global[:], w1[3 * P : 4 * P, :])
+        sources = (("receiver", receiver), ("sender", sender), ("edge", edge_attr))
+        x_halves = [[], []]
+        w1_blocks = []
+        for i in range(2):
+            for k, (name, source) in enumerate(sources):
+                x_block = held.tile([P, HALF], BF16, name=f"{name}_{i}")
+                nc.sync.dma_start(x_block[:], source[:, i * HALF : (i + 1) * HALF])
+                x_halves[i].append(x_block[:])
+                if i == 0:
+                    w1_block = held.tile([P, L], BF16, name=f"w1_{k}")
+                    nc.sync.dma_start(w1_block[:], w1[k * P : (k + 1) * P, :])
+                    w1_blocks.append(w1_block)
         w2_blocks = load_row_blocks(nc, held, w2, "w2")
         w3_blocks = load_row_blocks(nc, held, w3, "w3")
         w4_blocks = load_row_blocks(nc, held, w4, "w4")
+        offsets = lists.tile([P, N // 16], U16, name="offsets")
+        nc.sync.dma_start(offsets[:], offs)
         windows = load_row_blocks(nc, held, base, "window")
 
         identity = held.tile([P, P], FP32, name="identity")
@@ -108,7 +114,7 @@ def tile_edgemodel_b_kernel(
         for m in range(L // P):
             nc.tensor.matmul(
                 global_psum[:, m : m + 1],
-                w1_blocks[3][:, m * P : (m + 1) * P],
+                w1_global[:, m * P : (m + 1) * P],
                 global_column[:],
                 start=True,
                 stop=True,
@@ -123,8 +129,7 @@ def tile_edgemodel_b_kernel(
             nc.gpsimd.tensor_copy(wide[:], b4_columns[:, c : c + 1].to_broadcast([P, N]))
             b4_wide.append(wide)
 
-        x_halves = [[f[:, i * HALF : (i + 1) * HALF] for f in features] for i in range(2)]
-        h1 = hidden_layer(nc, banks, held, w1_blocks[0:3], x_halves, bias1, "h1")
+        h1 = hidden_layer(nc, banks, held, w1_blocks, x_halves, bias1, "h1")
         h2 = hidden_layer(nc, banks, held, w2_blocks, h1, bias_columns("b2", L // P), "h2")
         h3 = hidden_layer(nc, banks, held, w3_blocks, h2, bias_columns("b3", L // P), "h3")
 

@@ -16,6 +16,7 @@ L = 768
 C = 1024
 DI = 512
 HALF = 512
+WARM_UP = 6
 
 FLOPS = 2 * N * (DI * L + L * L + L * L + L * C)
 
@@ -63,6 +64,12 @@ def tile_edgemodel_b_kernel(
         tc.psum_pool(name="setup", bufs=1) as setup,
         tc.psum_pool(name="banks", bufs=6) as banks,
     ):
+        zeros = held.tile([P, HALF], BF16, name="zeros")
+        nc.vector.memset(zeros[:], 0.0)
+        unread = banks.tile([P, HALF], FP32, name="acc")
+        for repeat in range(WARM_UP):
+            nc.tensor.matmul(unread[:], zeros[:, 0:P], zeros[:], start=True, stop=True)
+
         global_column = held.tile([P, 1], BF16, name="global_column")
         nc.scalar.dma_start(global_column[:], global_attr)
 

@@ -1,5 +1,4 @@
 import concourse.mybir as mybir
-from concourse.masks import make_identity
 
 FP32 = mybir.dt.float32
 BF16 = mybir.dt.bfloat16
@@ -16,7 +15,7 @@ L = 768
 C = 1024
 DI = 512
 HALF = 512
-WARM_UP = 6
+WARM_UP = 3
 
 FLOPS = 2 * N * (DI * L + L * L + L * L + L * C)
 
@@ -29,6 +28,34 @@ def load_row_blocks(nc, pool, matrix, name):
         nc.sync.dma_start(block[:], matrix[k * P : (k + 1) * P, :])
         blocks.append(block)
     return blocks
+
+
+def empty_bank(nc, pool, acc, bias, m, name):
+    hidden = pool.tile([P, HALF], BF16, name=name)
+    if m % 2 == 0:
+        nc.scalar.activation(hidden[:], acc[:], RELU, bias=bias[:, m : m + 1])
+    else:
+        nc.vector.tensor_scalar(hidden[:], acc[:], bias[:, m : m + 1], 0.0, ADD, MAX)
+    return hidden[:]
+
+
+def first_layer(nc, banks, pool, weights, halves, bias, name):
+    outputs = []
+    for i, blocks in enumerate(halves):
+        accs = [banks.tile([P, HALF], FP32, name="acc") for m in range(L // P)]
+        for k, (weight, block) in enumerate(zip(weights, blocks)):
+            for m in range(L // P):
+                nc.tensor.matmul(
+                    accs[m][:],
+                    weight[:, m * P : (m + 1) * P],
+                    block,
+                    start=(k == 0),
+                    stop=(k == len(blocks) - 1),
+                )
+        outputs.append(
+            [empty_bank(nc, pool, accs[m], bias, m, f"{name}_{i}_{m}") for m in range(L // P)]
+        )
+    return outputs
 
 
 def hidden_layer(nc, banks, pool, weights, halves, bias, name):
@@ -45,12 +72,7 @@ def hidden_layer(nc, banks, pool, weights, halves, bias, name):
                     start=(k == 0),
                     stop=(k == len(blocks) - 1),
                 )
-            hidden = pool.tile([P, HALF], BF16, name=f"{name}_{i}_{m}")
-            if m % 2 == 0:
-                nc.scalar.activation(hidden[:], acc[:], RELU, bias=bias[:, m : m + 1])
-            else:
-                nc.vector.tensor_scalar(hidden[:], acc[:], bias[:, m : m + 1], 0.0, ADD, MAX)
-            outputs[i].append(hidden[:])
+            outputs[i].append(empty_bank(nc, pool, acc, bias, m, f"{name}_{i}_{m}"))
     return outputs
 
 
@@ -62,7 +84,7 @@ def tile_edgemodel_b_kernel(
         tc.tile_pool(name="lists", bufs=1) as lists,
         tc.tile_pool(name="held", bufs=1) as held,
         tc.psum_pool(name="setup", bufs=1) as setup,
-        tc.psum_pool(name="banks", bufs=6) as banks,
+        tc.psum_pool(name="banks", bufs=7) as banks,
     ):
         zeros = held.tile([P, HALF], BF16, name="zeros")
         nc.vector.memset(zeros[:], 0.0)
@@ -70,52 +92,39 @@ def tile_edgemodel_b_kernel(
         for repeat in range(WARM_UP):
             nc.tensor.matmul(unread[:], zeros[:, 0:P], zeros[:], start=True, stop=True)
 
+        table_in = held.tile([P, 1], BF16, name="table_in")
+        nc.scalar.activation(table_in[:], zeros[:, 0:1], RELU)
+
         global_column = held.tile([P, 1], BF16, name="global_column")
         nc.scalar.dma_start(global_column[:], global_attr)
 
-        bias_rows = held.tile([P, P], FP32, name="bias_rows")
-        nc.vector.memset(bias_rows[:], 0.0)
-        first_row = {}
-        rows_used = 0
+        bias = {}
         for name, vector in (("b1", b1), ("b2", b2), ("b3", b3), ("b4", b4)):
-            blocks = vector.shape[0] // P
-            nc.scalar.dma_start(
-                bias_rows[rows_used : rows_used + blocks, :],
-                vector.rearrange("(m p) o -> m (p o)", p=P),
-            )
-            first_row[name] = rows_used
-            rows_used += blocks
+            bias[name] = held.tile([P, vector.shape[0] // P], FP32, name=name)
+            nc.scalar.dma_start(bias[name][:], vector.rearrange("(m p) o -> p (m o)", p=P))
 
-        w1_global = held.tile([P, L], BF16, name="w1_global")
-        nc.sync.dma_start(w1_global[:], w1[3 * P : 4 * P, :])
         sources = (("receiver", receiver), ("sender", sender), ("edge", edge_attr))
         x_halves = [[], []]
         w1_blocks = []
-        for i in range(2):
-            for k, (name, source) in enumerate(sources):
-                x_block = held.tile([P, HALF], BF16, name=f"{name}_{i}")
-                nc.sync.dma_start(x_block[:], source[:, i * HALF : (i + 1) * HALF])
-                x_halves[i].append(x_block[:])
-                if i == 0:
-                    w1_block = held.tile([P, L], BF16, name=f"w1_{k}")
-                    nc.sync.dma_start(w1_block[:], w1[k * P : (k + 1) * P, :])
-                    w1_blocks.append(w1_block)
+        for k, (name, source) in enumerate(sources):
+            x_block = held.tile([P, HALF], BF16, name=f"{name}_0")
+            nc.sync.dma_start(x_block[:], source[:, 0:HALF])
+            x_halves[0].append(x_block[:])
+            w1_block = held.tile([P, L], BF16, name=f"w1_{k}")
+            nc.sync.dma_start(w1_block[:], w1[k * P : (k + 1) * P, :])
+            w1_blocks.append(w1_block)
+        w1_global = held.tile([P, L], BF16, name="w1_global")
+        nc.sync.dma_start(w1_global[:], w1[3 * P : 4 * P, :])
+        for name, source in sources:
+            x_block = held.tile([P, HALF], BF16, name=f"{name}_1")
+            nc.sync.dma_start(x_block[:], source[:, HALF:N])
+            x_halves[1].append(x_block[:])
         w2_blocks = load_row_blocks(nc, held, w2, "w2")
         w3_blocks = load_row_blocks(nc, held, w3, "w3")
         w4_blocks = load_row_blocks(nc, held, w4, "w4")
         offsets = lists.tile([P, N // 16], U16, name="offsets")
         nc.sync.dma_start(offsets[:], offs)
         windows = load_row_blocks(nc, held, base, "window")
-
-        identity = held.tile([P, P], FP32, name="identity")
-        make_identity(nc, identity[:])
-        bias_psum = setup.tile([P, P], FP32, name="bias_psum")
-        nc.tensor.transpose(bias_psum[:], bias_rows[:], identity[:])
-        bias = held.tile([P, P], FP32, name="bias")
-        nc.vector.tensor_copy(bias[:], bias_psum[:])
-
-        def bias_columns(name, count):
-            return bias[:, first_row[name] : first_row[name] + count]
 
         global_psum = setup.tile([P, L // P], FP32, name="global_psum")
         for m in range(L // P):
@@ -127,18 +136,17 @@ def tile_edgemodel_b_kernel(
                 stop=True,
             )
         bias1 = held.tile([P, L // P], FP32, name="bias1")
-        nc.vector.tensor_tensor(bias1[:], global_psum[:], bias_columns("b1", L // P), ADD)
+        nc.vector.tensor_tensor(bias1[:], global_psum[:], bias["b1"][:], ADD)
 
-        b4_columns = bias_columns("b4", C // P)
         b4_wide = []
         for c in range(C // P):
             wide = held.tile([P, N], FP32, name=f"b4_wide_{c}")
-            nc.gpsimd.tensor_copy(wide[:], b4_columns[:, c : c + 1].to_broadcast([P, N]))
+            nc.gpsimd.tensor_copy(wide[:], bias["b4"][:, c : c + 1].to_broadcast([P, N]))
             b4_wide.append(wide)
 
-        h1 = hidden_layer(nc, banks, held, w1_blocks, x_halves, bias1, "h1")
-        h2 = hidden_layer(nc, banks, held, w2_blocks, h1, bias_columns("b2", L // P), "h2")
-        h3 = hidden_layer(nc, banks, held, w3_blocks, h2, bias_columns("b3", L // P), "h3")
+        h1 = first_layer(nc, banks, held, w1_blocks, x_halves, bias1, "h1")
+        h2 = hidden_layer(nc, banks, held, w2_blocks, h1, bias["b2"], "h2")
+        h3 = hidden_layer(nc, banks, held, w3_blocks, h2, bias["b3"], "h3")
 
         for c in range(C // P):
             y = held.tile([P, N], FP32, name=f"y_{c}")

@@ -30,6 +30,12 @@ def load_row_blocks(nc, pool, matrix, name):
     return blocks
 
 
+def load_bias_columns(nc, pool, vector, name):
+    columns = pool.tile([P, vector.shape[0] // P], FP32, name=name)
+    nc.sync.dma_start(columns[:], vector.rearrange("(m p) o -> p (m o)", p=P))
+    return columns
+
+
 def empty_bank(nc, pool, acc, bias, m, name):
     hidden = pool.tile([P, HALF], BF16, name=name)
     if m % 2 == 0:
@@ -95,58 +101,62 @@ def tile_edgemodel_b_kernel(
         table_in = held.tile([P, 1], BF16, name="table_in")
         nc.scalar.activation(table_in[:], zeros[:, 0:1], RELU)
 
+        sources = (receiver, sender, edge_attr)
+        x_tiles = [
+            [held.tile([P, HALF], BF16, name=f"x_{i}_{k}") for k in range(len(sources))]
+            for i in range(2)
+        ]
+        w1_blocks = [held.tile([P, L], BF16, name=f"w1_{k}") for k in range(DI // P)]
         global_column = held.tile([P, 1], BF16, name="global_column")
-        nc.scalar.dma_start(global_column[:], global_attr)
 
-        bias = {}
-        for name, vector in (("b1", b1), ("b2", b2), ("b3", b3), ("b4", b4)):
-            bias[name] = held.tile([P, vector.shape[0] // P], FP32, name=name)
-            nc.scalar.dma_start(bias[name][:], vector.rearrange("(m p) o -> p (m o)", p=P))
+        def load_x(i, k):
+            nc.sync.dma_start(x_tiles[i][k][:], sources[k][:, i * HALF : (i + 1) * HALF])
 
-        sources = (("receiver", receiver), ("sender", sender), ("edge", edge_attr))
-        x_halves = [[], []]
-        w1_blocks = []
-        for k, (name, source) in enumerate(sources):
-            x_block = held.tile([P, HALF], BF16, name=f"{name}_0")
-            nc.sync.dma_start(x_block[:], source[:, 0:HALF])
-            x_halves[0].append(x_block[:])
-            w1_block = held.tile([P, L], BF16, name=f"w1_{k}")
-            nc.sync.dma_start(w1_block[:], w1[k * P : (k + 1) * P, :])
-            w1_blocks.append(w1_block)
-        w1_global = held.tile([P, L], BF16, name="w1_global")
-        nc.sync.dma_start(w1_global[:], w1[3 * P : 4 * P, :])
-        for name, source in sources:
-            x_block = held.tile([P, HALF], BF16, name=f"{name}_1")
-            nc.sync.dma_start(x_block[:], source[:, HALF:N])
-            x_halves[1].append(x_block[:])
+        def load_w1(k):
+            nc.sync.dma_start(w1_blocks[k][:], w1[k * P : (k + 1) * P, :])
+
+        load_x(0, 0)
+        load_w1(0)
+        nc.sync.dma_start(global_column[:], global_attr)
+        load_w1(len(sources))
+        b1_columns = load_bias_columns(nc, held, b1, "b1")
+        for k in range(1, len(sources)):
+            load_x(0, k)
+            load_w1(k)
+        for k in range(len(sources)):
+            load_x(1, k)
+        b2_columns = load_bias_columns(nc, held, b2, "b2")
         w2_blocks = load_row_blocks(nc, held, w2, "w2")
+        b3_columns = load_bias_columns(nc, held, b3, "b3")
         w3_blocks = load_row_blocks(nc, held, w3, "w3")
+        b4_columns = load_bias_columns(nc, held, b4, "b4")
         w4_blocks = load_row_blocks(nc, held, w4, "w4")
         offsets = lists.tile([P, N // 16], U16, name="offsets")
         nc.sync.dma_start(offsets[:], offs)
         windows = load_row_blocks(nc, held, base, "window")
+        x_halves = [[block[:] for block in half] for half in x_tiles]
 
         global_psum = setup.tile([P, L // P], FP32, name="global_psum")
         for m in range(L // P):
             nc.tensor.matmul(
                 global_psum[:, m : m + 1],
-                w1_global[:, m * P : (m + 1) * P],
+                w1_blocks[len(sources)][:, m * P : (m + 1) * P],
                 global_column[:],
                 start=True,
                 stop=True,
             )
         bias1 = held.tile([P, L // P], FP32, name="bias1")
-        nc.vector.tensor_tensor(bias1[:], global_psum[:], bias["b1"][:], ADD)
+        nc.vector.tensor_tensor(bias1[:], global_psum[:], b1_columns[:], ADD)
 
         b4_wide = []
         for c in range(C // P):
             wide = held.tile([P, N], FP32, name=f"b4_wide_{c}")
-            nc.gpsimd.tensor_copy(wide[:], bias["b4"][:, c : c + 1].to_broadcast([P, N]))
+            nc.gpsimd.tensor_copy(wide[:], b4_columns[:, c : c + 1].to_broadcast([P, N]))
             b4_wide.append(wide)
 
-        h1 = first_layer(nc, banks, held, w1_blocks, x_halves, bias1, "h1")
-        h2 = hidden_layer(nc, banks, held, w2_blocks, h1, bias["b2"], "h2")
-        h3 = hidden_layer(nc, banks, held, w3_blocks, h2, bias["b3"], "h3")
+        h1 = first_layer(nc, banks, held, w1_blocks[0 : len(sources)], x_halves, bias1, "h1")
+        h2 = hidden_layer(nc, banks, held, w2_blocks, h1, b2_columns, "h2")
+        h3 = hidden_layer(nc, banks, held, w3_blocks, h2, b3_columns, "h3")
 
         for c in range(C // P):
             y = held.tile([P, N], FP32, name=f"y_{c}")

@@ -98,9 +98,6 @@ def tile_edgemodel_b_kernel(
         for repeat in range(WARM_UP):
             nc.tensor.matmul(unread[:], zeros[:, 0:P], zeros[:], start=True, stop=True)
 
-        table_in = held.tile([P, 1], BF16, name="table_in")
-        nc.scalar.activation(table_in[:], zeros[:, 0:1], RELU)
-
         sources = (receiver, sender, edge_attr)
         x_tiles = [
             [held.tile([P, HALF], BF16, name=f"x_{i}_{k}") for k in range(len(sources))]

@@ -15,7 +15,6 @@ L = 768
 C = 1024
 DI = 512
 HALF = 512
-WARM_UP = 3
 
 FLOPS = 2 * N * (DI * L + L * L + L * L + L * C)
 
@@ -92,12 +91,6 @@ def tile_edgemodel_b_kernel(
         tc.psum_pool(name="setup", bufs=1) as setup,
         tc.psum_pool(name="banks", bufs=7) as banks,
     ):
-        zeros = held.tile([P, HALF], BF16, name="zeros")
-        nc.vector.memset(zeros[:], 0.0)
-        unread = banks.tile([P, HALF], FP32, name="acc")
-        for repeat in range(WARM_UP):
-            nc.tensor.matmul(unread[:], zeros[:, 0:P], zeros[:], start=True, stop=True)
-
         sources = (receiver, sender, edge_attr)
         x_tiles = [
             [held.tile([P, HALF], BF16, name=f"x_{i}_{k}") for k in range(len(sources))]

@@ -15,6 +15,7 @@ L = 768
 C = 1024
 DI = 512
 HALF = 512
+Y_PIECES = ((0, 512), (512, 384), (896, 128))
 
 FLOPS = 2 * N * (DI * L + L * L + L * L + L * C)
 
@@ -150,17 +151,18 @@ def tile_edgemodel_b_kernel(
 
         for c in range(C // P):
             y = held.tile([P, N], FP32, name=f"y_{c}")
-            for i in range(2):
+            for first, width in Y_PIECES:
+                i, inside = divmod(first, HALF)
                 acc = banks.tile([P, HALF], FP32, name="acc")
                 for k in range(L // P):
                     nc.tensor.matmul(
-                        acc[:],
+                        acc[:, 0:width],
                         w4_blocks[k][:, c * P : (c + 1) * P],
-                        h3[i][k],
+                        h3[i][k][:, inside : inside + width],
                         start=(k == 0),
                         stop=(k == L // P - 1),
                     )
-                nc.scalar.activation(y[:, i * HALF : (i + 1) * HALF], acc[:], COPY)
+                nc.scalar.activation(y[:, first : first + width], acc[:, 0:width], COPY)
             nc.vector.tensor_tensor(
                 windows[c][:].indirect(offsets[:]),
                 y[:],

@@ -45,25 +45,6 @@ def empty_bank(nc, pool, acc, bias, m, name):
     return hidden[:]
 
 
-def first_layer(nc, banks, pool, weights, halves, bias, name):
-    outputs = []
-    for i, blocks in enumerate(halves):
-        accs = [banks.tile([P, HALF], FP32, name="acc") for m in range(L // P)]
-        for k, (weight, block) in enumerate(zip(weights, blocks)):
-            for m in range(L // P):
-                nc.tensor.matmul(
-                    accs[m][:],
-                    weight[:, m * P : (m + 1) * P],
-                    block,
-                    start=(k == 0),
-                    stop=(k == len(blocks) - 1),
-                )
-        outputs.append(
-            [empty_bank(nc, pool, accs[m], bias, m, f"{name}_{i}_{m}") for m in range(L // P)]
-        )
-    return outputs
-
-
 def hidden_layer(nc, banks, pool, weights, halves, bias, name):
     outputs = []
     for i, blocks in enumerate(halves):
@@ -145,7 +126,7 @@ def tile_edgemodel_b_kernel(
             nc.gpsimd.tensor_copy(wide[:], b4_columns[:, c : c + 1].to_broadcast([P, N]))
             b4_wide.append(wide)
 
-        h1 = first_layer(nc, banks, held, w1_blocks[0 : len(sources)], x_halves, bias1, "h1")
+        h1 = hidden_layer(nc, banks, held, w1_blocks[0 : len(sources)], x_halves, bias1, "h1")
         h2 = hidden_layer(nc, banks, held, w2_blocks, h1, b2_columns, "h2")
         h3 = hidden_layer(nc, banks, held, w3_blocks, h2, b3_columns, "h3")
 

@@ -87,14 +87,16 @@ def tile_edgemodel_b_kernel(
         def load_w1(k):
             nc.sync.dma_start(w1_blocks[k][:], w1[k * P : (k + 1) * P, :])
 
-        load_x(0, 0)
-        load_w1(0)
+        nc.scalar.dma_start(x_tiles[0][0][:], sources[0][:, 0:HALF])
+        for columns in (slice(0, L // 2), slice(L // 2, L)):
+            nc.sync.dma_start(w1_blocks[0][:, columns], w1[0:P, columns])
+        load_x(0, 1)
+        load_w1(1)
         nc.sync.dma_start(global_column[:], global_attr)
         load_w1(len(sources))
         b1_columns = load_bias_columns(nc, held, b1, "b1")
-        for k in range(1, len(sources)):
-            load_x(0, k)
-            load_w1(k)
+        load_x(0, 2)
+        load_w1(2)
         for k in range(len(sources)):
             load_x(1, k)
         b2_columns = load_bias_columns(nc, held, b2, "b2")

@@ -12,6 +12,7 @@ P = 128
 N = 1024
 S = 2048
 L = 768
+GROUP = 3
 C = 1024
 DI = 512
 HALF = 512
@@ -30,15 +31,15 @@ def load_row_blocks(nc, pool, matrix, name):
     return blocks
 
 
-def load_bias_columns(nc, pool, vector, name):
+def load_bias_columns(pool, queue, vector, name):
     columns = pool.tile([P, vector.shape[0] // P], FP32, name=name)
-    nc.sync.dma_start(columns[:], vector.rearrange("(m p) o -> p (m o)", p=P))
+    queue.dma_start(columns[:], vector.rearrange("(m p) o -> p (m o)", p=P))
     return columns
 
 
 def empty_bank(nc, pool, acc, bias, m, name):
     hidden = pool.tile([P, HALF], BF16, name=name)
-    if m % 2 == 0:
+    if m % 2 == 1:
         nc.scalar.activation(hidden[:], acc[:], RELU, bias=bias[:, m : m + 1])
     else:
         nc.vector.tensor_scalar(hidden[:], acc[:], bias[:, m : m + 1], 0.0, ADD, MAX)
@@ -49,17 +50,20 @@ def hidden_layer(nc, banks, pool, weights, halves, bias, name):
     outputs = []
     for i, blocks in enumerate(halves):
         outputs.append([])
-        for m in range(L // P):
-            acc = banks.tile([P, HALF], FP32, name="acc")
+        for first in range(0, L // P, GROUP):
+            group = range(first, first + GROUP)
+            accs = [banks.tile([P, HALF], FP32, name="acc") for m in group]
             for k, (weight, block) in enumerate(zip(weights, blocks)):
-                nc.tensor.matmul(
-                    acc[:],
-                    weight[:, m * P : (m + 1) * P],
-                    block,
-                    start=(k == 0),
-                    stop=(k == len(blocks) - 1),
-                )
-            outputs[i].append(empty_bank(nc, pool, acc, bias, m, f"{name}_{i}_{m}"))
+                for m, acc in zip(group, accs):
+                    nc.tensor.matmul(
+                        acc[:],
+                        weight[:, m * P : (m + 1) * P],
+                        block,
+                        start=(k == 0),
+                        stop=(k == len(blocks) - 1),
+                    )
+            for m, acc in zip(group, accs):
+                outputs[i].append(empty_bank(nc, pool, acc, bias, m, f"{name}_{i}_{m}"))
     return outputs
 
 
@@ -81,29 +85,30 @@ def tile_edgemodel_b_kernel(
         w1_blocks = [held.tile([P, L], BF16, name=f"w1_{k}") for k in range(DI // P)]
         global_column = held.tile([P, 1], BF16, name="global_column")
 
-        def load_x(i, k):
-            nc.sync.dma_start(x_tiles[i][k][:], sources[k][:, i * HALF : (i + 1) * HALF])
+        def load_x(queue, i, k):
+            queue.dma_start(x_tiles[i][k][:], sources[k][:, i * HALF : (i + 1) * HALF])
 
-        def load_w1(k):
-            nc.sync.dma_start(w1_blocks[k][:], w1[k * P : (k + 1) * P, :])
+        def load_w1(k, columns):
+            nc.sync.dma_start(w1_blocks[k][:, columns], w1[k * P : (k + 1) * P, columns])
 
-        nc.scalar.dma_start(x_tiles[0][0][:], sources[0][:, 0:HALF])
-        for columns in (slice(0, L // 2), slice(L // 2, L)):
-            nc.sync.dma_start(w1_blocks[0][:, columns], w1[0:P, columns])
-        load_x(0, 1)
-        load_w1(1)
-        nc.sync.dma_start(global_column[:], global_attr)
-        load_w1(len(sources))
-        b1_columns = load_bias_columns(nc, held, b1, "b1")
-        load_x(0, 2)
-        load_w1(2)
+        first_group, second_group = slice(0, GROUP * P), slice(GROUP * P, L)
+        load_x(nc.scalar, 0, 0)
+        b1_columns = load_bias_columns(held, nc.scalar, b1, "b1")
+        nc.scalar.dma_start(global_column[:], global_attr)
+        load_w1(0, first_group)
+        for k in range(1, len(sources)):
+            load_x(nc.sync, 0, k)
+            load_w1(k, first_group)
         for k in range(len(sources)):
-            load_x(1, k)
-        b2_columns = load_bias_columns(nc, held, b2, "b2")
+            load_w1(k, second_group)
+        load_w1(len(sources), slice(0, L))
+        for k in range(len(sources)):
+            load_x(nc.sync, 1, k)
+        b2_columns = load_bias_columns(held, nc.sync, b2, "b2")
         w2_blocks = load_row_blocks(nc, held, w2, "w2")
-        b3_columns = load_bias_columns(nc, held, b3, "b3")
+        b3_columns = load_bias_columns(held, nc.sync, b3, "b3")
         w3_blocks = load_row_blocks(nc, held, w3, "w3")
-        b4_columns = load_bias_columns(nc, held, b4, "b4")
+        b4_columns = load_bias_columns(held, nc.sync, b4, "b4")
         w4_blocks = load_row_blocks(nc, held, w4, "w4")
         offsets = lists.tile([P, N // 16], U16, name="offsets")
         nc.sync.dma_start(offsets[:], offs)

@@ -13,6 +13,7 @@ N = 1024
 S = 2048
 L = 768
 GROUP = 3
+WIDTH = GROUP * P
 C = 1024
 DI = 512
 HALF = 512
@@ -31,10 +32,28 @@ def load_row_blocks(nc, pool, matrix, name):
     return blocks
 
 
-def load_bias_columns(pool, queue, vector, name):
-    columns = pool.tile([P, vector.shape[0] // P], FP32, name=name)
-    queue.dma_start(columns[:], vector.rearrange("(m p) o -> p (m o)", p=P))
+def load_hidden_rows(nc, pool, matrix, name):
+    rows = matrix.rearrange("(g p j) m -> g j p m", p=P, j=GROUP)
+    blocks = []
+    for k in range(L // P):
+        block = pool.tile([P, matrix.shape[1]], matrix.dtype, name=f"{name}_{k}")
+        nc.sync.dma_start(block[:], rows[k // GROUP, k % GROUP])
+        blocks.append(block)
+    return blocks
+
+
+def load_hidden_bias(nc, pool, vector, name):
+    columns = pool.tile([P, L // P], FP32, name=name)
+    nc.sync.dma_start(
+        columns[:].rearrange("p (g j) -> p g j", j=GROUP),
+        vector.rearrange("(g p j) o -> p g (j o)", p=P, j=GROUP),
+    )
     return columns
+
+
+def hidden_columns(weight, m):
+    group, j = divmod(m, GROUP)
+    return weight[:, group * WIDTH + j : (group + 1) * WIDTH : GROUP]
 
 
 def empty_bank(nc, pool, acc, bias, m, name):
@@ -57,7 +76,7 @@ def hidden_layer(nc, banks, pool, weights, halves, bias, name):
                 for m, acc in zip(group, accs):
                     nc.tensor.matmul(
                         acc[:],
-                        weight[:, m * P : (m + 1) * P],
+                        hidden_columns(weight, m),
                         block,
                         start=(k == 0),
                         stop=(k == len(blocks) - 1),
@@ -91,25 +110,27 @@ def tile_edgemodel_b_kernel(
         def load_w1(k, columns):
             nc.sync.dma_start(w1_blocks[k][:, columns], w1[k * P : (k + 1) * P, columns])
 
-        first_group, second_group = slice(0, GROUP * P), slice(GROUP * P, L)
+        first_group, second_group = slice(0, WIDTH), slice(WIDTH, L)
         load_x(nc.scalar, 0, 0)
-        b1_columns = load_bias_columns(held, nc.scalar, b1, "b1")
-        nc.scalar.dma_start(global_column[:], global_attr)
         load_w1(0, first_group)
-        for k in range(1, len(sources)):
-            load_x(nc.sync, 0, k)
-            load_w1(k, first_group)
+        load_x(nc.sync, 0, 1)
+        load_w1(1, first_group)
+        nc.sync.dma_start(global_column[:], global_attr)
+        load_w1(len(sources), slice(0, L))
+        b1_columns = load_hidden_bias(nc, held, b1, "b1")
+        load_x(nc.sync, 0, 2)
+        load_w1(2, first_group)
         for k in range(len(sources)):
             load_w1(k, second_group)
-        load_w1(len(sources), slice(0, L))
         for k in range(len(sources)):
             load_x(nc.sync, 1, k)
-        b2_columns = load_bias_columns(held, nc.sync, b2, "b2")
-        w2_blocks = load_row_blocks(nc, held, w2, "w2")
-        b3_columns = load_bias_columns(held, nc.sync, b3, "b3")
-        w3_blocks = load_row_blocks(nc, held, w3, "w3")
-        b4_columns = load_bias_columns(held, nc.sync, b4, "b4")
-        w4_blocks = load_row_blocks(nc, held, w4, "w4")
+        b2_columns = load_hidden_bias(nc, held, b2, "b2")
+        w2_blocks = load_hidden_rows(nc, held, w2, "w2")
+        b3_columns = load_hidden_bias(nc, held, b3, "b3")
+        w3_blocks = load_hidden_rows(nc, held, w3, "w3")
+        b4_columns = held.tile([P, C // P], FP32, name="b4")
+        nc.sync.dma_start(b4_columns[:], b4.rearrange("(c p) o -> p (c o)", p=P))
+        w4_blocks = load_hidden_rows(nc, held, w4, "w4")
         offsets = lists.tile([P, N // 16], U16, name="offsets")
         nc.sync.dma_start(offsets[:], offs)
         windows = load_row_blocks(nc, held, base, "window")
@@ -119,7 +140,7 @@ def tile_edgemodel_b_kernel(
         for m in range(L // P):
             nc.tensor.matmul(
                 global_psum[:, m : m + 1],
-                w1_blocks[len(sources)][:, m * P : (m + 1) * P],
+                hidden_columns(w1_blocks[len(sources)], m),
                 global_column[:],
                 start=True,
                 stop=True,

@@ -178,4 +178,8 @@ def tile_edgemodel_b_kernel(
                 b4_wide[c][:],
                 ADD,
             )
-            nc.sync.dma_start(out[c * P : (c + 1) * P, :], windows[c][:])
+            if c < C // P - 1:
+                nc.sync.dma_start(out[c * P : (c + 1) * P, :], windows[c][:])
+            else:
+                for queue, columns in ((nc.sync, slice(0, S // 2)), (nc.scalar, slice(S // 2, S))):
+                    queue.dma_start(out[c * P : (c + 1) * P, columns], windows[c][:, columns])

@@ -12,7 +12,7 @@ P = 128
 N = 1024
 S = 2048
 L = 768
-GROUP = 3
+GROUP = 2
 WIDTH = GROUP * P
 C = 1024
 DI = 512
@@ -110,7 +110,7 @@ def tile_edgemodel_b_kernel(
         def load_w1(k, columns):
             nc.sync.dma_start(w1_blocks[k][:, columns], w1[k * P : (k + 1) * P, columns])
 
-        first_group, second_group = slice(0, WIDTH), slice(WIDTH, L)
+        first_group, other_groups = slice(0, WIDTH), slice(WIDTH, L)
         load_x(nc.scalar, 0, 0)
         load_w1(0, first_group)
         load_x(nc.sync, 0, 1)
@@ -121,7 +121,7 @@ def tile_edgemodel_b_kernel(
         load_x(nc.sync, 0, 2)
         load_w1(2, first_group)
         for k in range(len(sources)):
-            load_w1(k, second_group)
+            load_w1(k, other_groups)
         for k in range(len(sources)):
             load_x(nc.sync, 1, k)
         b2_columns = load_hidden_bias(nc, held, b2, "b2")
@@ -178,8 +178,4 @@ def tile_edgemodel_b_kernel(
                 b4_wide[c][:],
                 ADD,
             )
-            if c < C // P - 1:
-                nc.sync.dma_start(out[c * P : (c + 1) * P, :], windows[c][:])
-            else:
-                for queue, columns in ((nc.sync, slice(0, S // 2)), (nc.scalar, slice(S // 2, S))):
-                    queue.dma_start(out[c * P : (c + 1) * P, columns], windows[c][:, columns])
+            nc.sync.dma_start(out[c * P : (c + 1) * P, :], windows[c][:])

@@ -12,6 +12,7 @@ P = 128
 N = 1024
 S = 2048
 L = 768
+LB = L // P
 GROUP = 2
 WIDTH = GROUP * P
 C = 1024
@@ -35,15 +36,15 @@ def load_row_blocks(nc, pool, matrix, name):
 def load_hidden_rows(nc, pool, matrix, name):
     rows = matrix.rearrange("(g p j) m -> g j p m", p=P, j=GROUP)
     blocks = []
-    for k in range(L // P):
+    for k in range(LB):
         block = pool.tile([P, matrix.shape[1]], matrix.dtype, name=f"{name}_{k}")
         nc.sync.dma_start(block[:], rows[k // GROUP, k % GROUP])
-        blocks.append(block)
+        blocks.append(block[:])
     return blocks
 
 
 def load_hidden_bias(nc, pool, vector, name):
-    columns = pool.tile([P, L // P], FP32, name=name)
+    columns = pool.tile([P, LB], FP32, name=name)
     nc.sync.dma_start(
         columns[:].rearrange("p (g j) -> p g j", j=GROUP),
         vector.rearrange("(g p j) o -> p g (j o)", p=P, j=GROUP),
@@ -65,15 +66,15 @@ def empty_bank(nc, pool, acc, bias, m, name):
     return hidden[:]
 
 
-def hidden_layer(nc, banks, pool, weights, halves, bias, name):
+def hidden_layer(nc, banks, pool, weights, halves, bias, name, abreast=(1, 1)):
     outputs = []
     for i, blocks in enumerate(halves):
         outputs.append([])
-        for first in range(0, L // P, GROUP):
-            group = range(first, first + GROUP)
-            accs = [banks.tile([P, HALF], FP32, name="acc") for m in group]
+        for first in range(0, LB, abreast[i]):
+            row = range(first, first + abreast[i])
+            accs = [banks.tile([P, HALF], FP32, name="acc") for m in row]
             for k, (weight, block) in enumerate(zip(weights, blocks)):
-                for m, acc in zip(group, accs):
+                for m, acc in zip(row, accs):
                     nc.tensor.matmul(
                         acc[:],
                         hidden_columns(weight, m),
@@ -81,7 +82,7 @@ def hidden_layer(nc, banks, pool, weights, halves, bias, name):
                         start=(k == 0),
                         stop=(k == len(blocks) - 1),
                     )
-            for m, acc in zip(group, accs):
+            for m, acc in zip(row, accs):
                 outputs[i].append(empty_bank(nc, pool, acc, bias, m, f"{name}_{i}_{m}"))
     return outputs
 
@@ -101,27 +102,23 @@ def tile_edgemodel_b_kernel(
             [held.tile([P, HALF], BF16, name=f"x_{i}_{k}") for k in range(len(sources))]
             for i in range(2)
         ]
-        w1_blocks = [held.tile([P, L], BF16, name=f"w1_{k}") for k in range(DI // P)]
+        w1_tile = held.tile([P, DI // P, L], BF16, name="w1")
+        w1_blocks = [w1_tile[:, k, :] for k in range(DI // P)]
+        w1_rows = w1.rearrange("(k p) l -> p k l", p=P)
         global_column = held.tile([P, 1], BF16, name="global_column")
 
         def load_x(queue, i, k):
             queue.dma_start(x_tiles[i][k][:], sources[k][:, i * HALF : (i + 1) * HALF])
 
-        def load_w1(k, columns):
-            nc.sync.dma_start(w1_blocks[k][:, columns], w1[k * P : (k + 1) * P, columns])
-
-        first_group, other_groups = slice(0, WIDTH), slice(WIDTH, L)
         load_x(nc.scalar, 0, 0)
-        load_w1(0, first_group)
+        nc.sync.dma_start(w1_tile[:, 0, 0:WIDTH], w1_rows[:, 0, 0:WIDTH])
+        nc.sync.dma_start(w1_tile[:, 0, WIDTH:L], w1_rows[:, 0, WIDTH:L])
         load_x(nc.sync, 0, 1)
-        load_w1(1, first_group)
-        nc.sync.dma_start(global_column[:], global_attr)
-        load_w1(len(sources), slice(0, L))
-        b1_columns = load_hidden_bias(nc, held, b1, "b1")
+        nc.sync.dma_start(w1_blocks[1], w1_rows[:, 1, :])
         load_x(nc.sync, 0, 2)
-        load_w1(2, first_group)
-        for k in range(len(sources)):
-            load_w1(k, other_groups)
+        nc.sync.dma_start(w1_tile[:, 2:4, :], w1_rows[:, 2:4, :])
+        nc.sync.dma_start(global_column[:], global_attr)
+        b1_columns = load_hidden_bias(nc, held, b1, "b1")
         for k in range(len(sources)):
             load_x(nc.sync, 1, k)
         b2_columns = load_hidden_bias(nc, held, b2, "b2")
@@ -136,8 +133,8 @@ def tile_edgemodel_b_kernel(
         windows = load_row_blocks(nc, held, base, "window")
         x_halves = [[block[:] for block in half] for half in x_tiles]
 
-        global_psum = setup.tile([P, L // P], FP32, name="global_psum")
-        for m in range(L // P):
+        global_psum = setup.tile([P, LB], FP32, name="global_psum")
+        for m in range(LB):
             nc.tensor.matmul(
                 global_psum[:, m : m + 1],
                 hidden_columns(w1_blocks[len(sources)], m),
@@ -145,7 +142,7 @@ def tile_edgemodel_b_kernel(
                 start=True,
                 stop=True,
             )
-        bias1 = held.tile([P, L // P], FP32, name="bias1")
+        bias1 = held.tile([P, LB], FP32, name="bias1")
         nc.vector.tensor_tensor(bias1[:], global_psum[:], b1_columns[:], ADD)
 
         b4_wide = []
@@ -154,7 +151,8 @@ def tile_edgemodel_b_kernel(
             nc.gpsimd.tensor_copy(wide[:], b4_columns[:, c : c + 1].to_broadcast([P, N]))
             b4_wide.append(wide)
 
-        h1 = hidden_layer(nc, banks, held, w1_blocks[0 : len(sources)], x_halves, bias1, "h1")
+        w1_of_x = w1_blocks[0 : len(sources)]
+        h1 = hidden_layer(nc, banks, held, w1_of_x, x_halves, bias1, "h1", abreast=(LB, 1))
         h2 = hidden_layer(nc, banks, held, w2_blocks, h1, b2_columns, "h2")
         h3 = hidden_layer(nc, banks, held, w3_blocks, h2, b3_columns, "h3")
 
@@ -163,13 +161,13 @@ def tile_edgemodel_b_kernel(
             for first, width in Y_PIECES:
                 i, inside = divmod(first, HALF)
                 acc = banks.tile([P, HALF], FP32, name="acc")
-                for k in range(L // P):
+                for k in range(LB):
                     nc.tensor.matmul(
                         acc[:, 0:width],
                         w4_blocks[k][:, c * P : (c + 1) * P],
                         h3[i][k][:, inside : inside + width],
                         start=(k == 0),
-                        stop=(k == L // P - 1),
+                        stop=(k == LB - 1),
                     )
                 nc.scalar.activation(y[:, first : first + width], acc[:, 0:width], COPY)
             nc.vector.tensor_tensor(

@@ -145,15 +145,16 @@ def tile_edgemodel_b_kernel(
         bias1 = held.tile([P, LB], FP32, name="bias1")
         nc.vector.tensor_tensor(bias1[:], global_psum[:], b1_columns[:], ADD)
 
-        b4_wide = []
-        for c in range(C // P):
-            wide = held.tile([P, N], FP32, name=f"b4_wide_{c}")
-            nc.gpsimd.tensor_copy(wide[:], b4_columns[:, c : c + 1].to_broadcast([P, N]))
-            b4_wide.append(wide)
-
         w1_of_x = w1_blocks[0 : len(sources)]
         h1 = hidden_layer(nc, banks, held, w1_of_x, x_halves, bias1, "h1", abreast=(LB, 1))
         h2 = hidden_layer(nc, banks, held, w2_blocks, h1, b2_columns, "h2")
+
+        b4_wide = []
+        for c in range(C // P):
+            wide = held.tile([P, N], FP32, name=f"b4_wide_{c}")
+            nc.scalar.activation(wide[:], b4_columns[:, c : c + 1].to_broadcast([P, N]), COPY)
+            b4_wide.append(wide)
+
         h3 = hidden_layer(nc, banks, held, w3_blocks, h2, b3_columns, "h3")
 
         for c in range(C // P):

import concourse.mybir as mybir

FP32 = mybir.dt.float32
BF16 = mybir.dt.bfloat16
U16 = mybir.dt.uint16
ADD = mybir.AluOpType.add
MAX = mybir.AluOpType.max
RELU = mybir.ActivationFunctionType.Relu
COPY = mybir.ActivationFunctionType.Copy

P = 128
N = 1024
S = 2048
L = 768
LB = L // P
GROUP = 2
WIDTH = GROUP * P
C = 1024
DI = 512
HALF = 512
Y_PIECES = ((0, 512), (512, 384), (896, 128))

FLOPS = 2 * N * (DI * L + L * L + L * L + L * C)


def load_row_blocks(nc, pool, matrix, name):
    rows, columns = matrix.shape
    blocks = []
    for k in range(rows // P):
        block = pool.tile([P, columns], matrix.dtype, name=f"{name}_{k}")
        nc.sync.dma_start(block[:], matrix[k * P : (k + 1) * P, :])
        blocks.append(block)
    return blocks


def load_hidden_rows(nc, pool, matrix, name):
    rows = matrix.rearrange("(g p j) m -> g j p m", p=P, j=GROUP)
    blocks = []
    for k in range(LB):
        block = pool.tile([P, matrix.shape[1]], matrix.dtype, name=f"{name}_{k}")
        nc.sync.dma_start(block[:], rows[k // GROUP, k % GROUP])
        blocks.append(block[:])
    return blocks


def load_hidden_bias(nc, pool, vector, name):
    columns = pool.tile([P, LB], FP32, name=name)
    nc.sync.dma_start(
        columns[:].rearrange("p (g j) -> p g j", j=GROUP),
        vector.rearrange("(g p j) o -> p g (j o)", p=P, j=GROUP),
    )
    return columns


def hidden_columns(weight, m):
    group, j = divmod(m, GROUP)
    return weight[:, group * WIDTH + j : (group + 1) * WIDTH : GROUP]


def empty_bank(nc, pool, acc, bias, m, name):
    hidden = pool.tile([P, HALF], BF16, name=name)
    if m % 2 == 1:
        nc.scalar.activation(hidden[:], acc[:], RELU, bias=bias[:, m : m + 1])
    else:
        nc.vector.tensor_scalar(hidden[:], acc[:], bias[:, m : m + 1], 0.0, ADD, MAX)
    return hidden[:]


def hidden_layer(nc, banks, pool, weights, halves, bias, name, abreast=(1, 1)):
    outputs = []
    for i, blocks in enumerate(halves):
        outputs.append([])
        for first in range(0, LB, abreast[i]):
            row = range(first, first + abreast[i])
            accs = [banks.tile([P, HALF], FP32, name="acc") for m in row]
            for k, (weight, block) in enumerate(zip(weights, blocks)):
                for m, acc in zip(row, accs):
                    nc.tensor.matmul(
                        acc[:],
                        hidden_columns(weight, m),
                        block,
                        start=(k == 0),
                        stop=(k == len(blocks) - 1),
                    )
            for m, acc in zip(row, accs):
                outputs[i].append(empty_bank(nc, pool, acc, bias, m, f"{name}_{i}_{m}"))
    return outputs


def tile_edgemodel_b_kernel(
    tc, base, receiver, sender, edge_attr, global_attr, w1, b1, w2, b2, w3, b3, w4, b4, offs, out
):
    nc = tc.nc
    with (
        tc.tile_pool(name="lists", bufs=1) as lists,
        tc.tile_pool(name="held", bufs=1) as held,
        tc.psum_pool(name="setup", bufs=1) as setup,
        tc.psum_pool(name="banks", bufs=7) as banks,
    ):
        sources = (receiver, sender, edge_attr)
        x_tiles = [
            [held.tile([P, HALF], BF16, name=f"x_{i}_{k}") for k in range(len(sources))]
            for i in range(2)
        ]
        w1_tile = held.tile([P, DI // P, L], BF16, name="w1")
        w1_blocks = [w1_tile[:, k, :] for k in range(DI // P)]
        w1_rows = w1.rearrange("(k p) l -> p k l", p=P)
        global_column = held.tile([P, 1], BF16, name="global_column")

        def load_x(queue, i, k):
            queue.dma_start(x_tiles[i][k][:], sources[k][:, i * HALF : (i + 1) * HALF])

        load_x(nc.scalar, 0, 0)
        nc.sync.dma_start(w1_tile[:, 0, 0:WIDTH], w1_rows[:, 0, 0:WIDTH])
        nc.sync.dma_start(w1_tile[:, 0, WIDTH:L], w1_rows[:, 0, WIDTH:L])
        load_x(nc.sync, 0, 1)
        nc.sync.dma_start(w1_blocks[1], w1_rows[:, 1, :])
        load_x(nc.sync, 0, 2)
        nc.sync.dma_start(w1_tile[:, 2:4, :], w1_rows[:, 2:4, :])
        nc.sync.dma_start(global_column[:], global_attr)
        b1_columns = load_hidden_bias(nc, held, b1, "b1")
        for k in range(len(sources)):
            load_x(nc.sync, 1, k)
        b2_columns = load_hidden_bias(nc, held, b2, "b2")
        w2_blocks = load_hidden_rows(nc, held, w2, "w2")
        b3_columns = load_hidden_bias(nc, held, b3, "b3")
        w3_blocks = load_hidden_rows(nc, held, w3, "w3")
        b4_columns = held.tile([P, C // P], FP32, name="b4")
        nc.sync.dma_start(b4_columns[:], b4.rearrange("(c p) o -> p (c o)", p=P))
        w4_blocks = load_hidden_rows(nc, held, w4, "w4")
        offsets = lists.tile([P, N // 16], U16, name="offsets")
        nc.sync.dma_start(offsets[:], offs)
        windows = load_row_blocks(nc, held, base, "window")
        x_halves = [[block[:] for block in half] for half in x_tiles]

        global_psum = setup.tile([P, LB], FP32, name="global_psum")
        for m in range(LB):
            nc.tensor.matmul(
                global_psum[:, m : m + 1],
                hidden_columns(w1_blocks[len(sources)], m),
                global_column[:],
                start=True,
                stop=True,
            )
        bias1 = held.tile([P, LB], FP32, name="bias1")
        nc.vector.tensor_tensor(bias1[:], global_psum[:], b1_columns[:], ADD)

        w1_of_x = w1_blocks[0 : len(sources)]
        h1 = hidden_layer(nc, banks, held, w1_of_x, x_halves, bias1, "h1", abreast=(LB, 1))
        h2 = hidden_layer(nc, banks, held, w2_blocks, h1, b2_columns, "h2")

        b4_wide = []
        for c in range(C // P):
            wide = held.tile([P, N], FP32, name=f"b4_wide_{c}")
            nc.scalar.activation(wide[:], b4_columns[:, c : c + 1].to_broadcast([P, N]), COPY)
            b4_wide.append(wide)

        h3 = hidden_layer(nc, banks, held, w3_blocks, h2, b3_columns, "h3")

        for c in range(C // P):
            y = held.tile([P, N], FP32, name=f"y_{c}")
            for first, width in Y_PIECES:
                i, inside = divmod(first, HALF)
                acc = banks.tile([P, HALF], FP32, name="acc")
                for k in range(LB):
                    nc.tensor.matmul(
                        acc[:, 0:width],
                        w4_blocks[k][:, c * P : (c + 1) * P],
                        h3[i][k][:, inside : inside + width],
                        start=(k == 0),
                        stop=(k == LB - 1),
                    )
                nc.scalar.activation(y[:, first : first + width], acc[:, 0:width], COPY)
            nc.vector.tensor_tensor(
                windows[c][:].indirect(offsets[:]),
                y[:],
                b4_wide[c][:],
                ADD,
            )
            nc.sync.dma_start(out[c * P : (c + 1) * P, :], windows[c][:])
